import numpy as np
import ml_dtypes

BF16 = ml_dtypes.bfloat16


def bf(x):
    return np.asarray(x, np.float32).astype(BF16)


def f32(x):
    return np.asarray(x, np.float32)


def f64(x):
    return np.asarray(x).astype(np.float64)


def striped(idx):
    return np.tile(idx.reshape(-1, 16).T, (8, 1))


S, D, M, N = 1024, 128, 256, 512
BN_EPS = 1e-5


def setup_inputs():
    return {"table": bf(np.random.standard_normal((D, S))), "w": bf(np.random.standard_normal((D, M)) / np.sqrt(D)), "b": f32(0.1 * np.random.standard_normal((M, 1))), "gain": f32(1.0 + 0.1 * np.random.standard_normal((M, 1))), "shift": f32(0.1 * np.random.standard_normal((M, 1))), "offs": striped(np.random.permutation(np.tile(np.arange(S), 2))[:N])}


def reference(table, w, b, gain, shift, offs):
    idx = offs[:16].T.reshape(-1)
    h = np.maximum(f64(w).T @ f64(table)[:, idx] + f64(b), 0.0)
    mu = h.mean(axis=1, keepdims=True)
    var = ((h - mu) ** 2).mean(axis=1, keepdims=True)
    return f64(gain) * (h - mu) / np.sqrt(var + BN_EPS) + f64(shift)

@@ -1,0 +1,75 @@
+import concourse.mybir as mybir
+
+F32 = mybir.dt.float32
+BF16 = mybir.dt.bfloat16
+U16 = mybir.dt.uint16
+ACT = mybir.ActivationFunctionType
+ALU = mybir.AluOpType
+
+P = 128
+S = 1024
+M = 256
+N = 512
+BLOCKS = M // P
+BN_EPS = 1e-5
+
+FLOPS = 2 * P * M * N
+
+
+def tile_criteomlp_kernel(tc, table, w, b, gain, shift, offs, out):
+    nc = tc.nc
+    with (
+        tc.tile_pool(name="held", bufs=1) as held,
+        tc.tile_pool(name="work", bufs=2) as work,
+        tc.psum_pool(name="psum", bufs=2) as psum,
+    ):
+        offsets = held.tile([P, N // 16], U16, name="offsets")
+        nc.sync.dma_start(offsets[:], offs)
+        table_sb = held.tile([P, S], BF16, name="table_sb")
+        nc.sync.dma_start(table_sb[:], table)
+        w_sb = held.tile([P, M], BF16, name="w_sb")
+        nc.scalar.dma_start(w_sb[:], w)
+
+        b_sb = held.tile([P, BLOCKS], F32, name="b_sb")
+        gain_sb = held.tile([P, BLOCKS], F32, name="gain_sb")
+        shift_sb = held.tile([P, BLOCKS], F32, name="shift_sb")
+        with nc.allow_non_contiguous_dma(reason="one float32 to a partition, 256 in all"):
+            nc.scalar.dma_start(b_sb[:], b.rearrange("(t p) o -> p (t o)", p=P))
+            nc.gpsimd.dma_start(gain_sb[:], gain.rearrange("(t p) o -> p (t o)", p=P))
+            nc.gpsimd.dma_start(shift_sb[:], shift.rearrange("(t p) o -> p (t o)", p=P))
+
+        eps = held.tile([P, 1], F32, name="eps")
+        nc.vector.memset(eps[:], BN_EPS)
+
+        for t in range(BLOCKS):
+            product = psum.tile([P, N], F32, name="product")
+            nc.tensor.matmul(
+                product[:],
+                w_sb[:, t * P : (t + 1) * P],
+                table_sb[:].indirect(offsets[:]),
+                start=True,
+                stop=True,
+            )
+
+            h = work.tile([P, N], F32, name="h")
+            nc.scalar.activation(h[:], product[:], ACT.Relu, bias=b_sb[:, t : t + 1])
+
+            stats = work.tile([P, 6], F32, name="stats")
+            nc.vector.bn_stats(stats[:], h[:])
+            mean_var = work.tile([P, 2], F32, name="mean_var")
+            nc.vector.bn_aggr(mean_var[:], stats[:])
+            mean = mean_var[:, 0:1]
+            var = mean_var[:, 1:2]
+
+            std = work.tile([P, 1], F32, name="std")
+            nc.scalar.activation(std[:], var, ACT.Sqrt, bias=eps[:])
+            slope = work.tile([P, 1], F32, name="slope")
+            nc.vector.reciprocal(slope[:], std[:])
+            nc.vector.tensor_mul(slope[:], slope[:], gain_sb[:, t : t + 1])
+            drop = work.tile([P, 1], F32, name="drop")
+            nc.vector.scalar_tensor_tensor(
+                drop[:], mean, slope[:], shift_sb[:, t : t + 1], ALU.mult, ALU.subtract
+            )
+            y = work.tile([P, N], F32, name="y")
+            nc.vector.tensor_scalar(y[:], h[:], slope[:], drop[:], ALU.mult, ALU.subtract)
+            nc.sync.dma_start(out[t * P : (t + 1) * P, :], y[:])

@@ -35,11 +35,14 @@ def tile_criteomlp_kernel(tc, table, w, b, gain, shift, offs, out):
         shift_sb = held.tile([P, BLOCKS], F32, name="shift_sb")
         with nc.allow_non_contiguous_dma(reason="one float32 to a partition, 256 in all"):
             nc.scalar.dma_start(b_sb[:], b.rearrange("(t p) o -> p (t o)", p=P))
-            nc.gpsimd.dma_start(gain_sb[:], gain.rearrange("(t p) o -> p (t o)", p=P))
-            nc.gpsimd.dma_start(shift_sb[:], shift.rearrange("(t p) o -> p (t o)", p=P))
+            nc.scalar.dma_start(gain_sb[:], gain.rearrange("(t p) o -> p (t o)", p=P))
+            nc.scalar.dma_start(shift_sb[:], shift.rearrange("(t p) o -> p (t o)", p=P))
 
         eps = held.tile([P, 1], F32, name="eps")
         nc.vector.memset(eps[:], BN_EPS)
+
+        first_sqrt = held.tile([P, 1], F32, name="first_sqrt")
+        nc.scalar.activation(first_sqrt[:], eps[:], ACT.Sqrt)
 
         for t in range(BLOCKS):
             product = psum.tile([P, N], F32, name="product")

@@ -11,7 +11,11 @@ S = 1024
 M = 256
 N = 512
 BLOCKS = M // P
+PIECES = 2
+PIECE = N // PIECES
+PIECE_OFFSET_COLUMNS = PIECE // 16
 BN_EPS = 1e-5
+VECTOR_COLUMNS = (2 * N // 3) // 16 * 16
 
 FLOPS = 2 * P * M * N
 
@@ -20,8 +24,8 @@ def tile_criteomlp_kernel(tc, table, w, b, gain, shift, offs, out):
     nc = tc.nc
     with (
         tc.tile_pool(name="held", bufs=1) as held,
-        tc.tile_pool(name="work", bufs=2) as work,
-        tc.psum_pool(name="psum", bufs=2) as psum,
+        tc.tile_pool(name="blocks", bufs=BLOCKS) as blocks,
+        tc.psum_pool(name="psum", bufs=BLOCKS * PIECES) as psum,
     ):
         offsets = held.tile([P, N // 16], U16, name="offsets")
         nc.sync.dma_start(offsets[:], offs)
@@ -41,38 +45,58 @@ def tile_criteomlp_kernel(tc, table, w, b, gain, shift, offs, out):
         eps = held.tile([P, 1], F32, name="eps")
         nc.vector.memset(eps[:], BN_EPS)
 
-        first_sqrt = held.tile([P, 1], F32, name="first_sqrt")
-        nc.scalar.activation(first_sqrt[:], eps[:], ACT.Sqrt)
+        first_call = held.tile([P, 1], F32, name="first_call")
+        nc.scalar.activation(first_call[:], eps[:], ACT.Abs_reciprocal_sqrt)
+
+        mean_var = held.tile([P, BLOCKS, 2], F32, name="mean_var")
+        hidden = []
+        for t in range(BLOCKS):
+            h = blocks.tile([P, N], F32, name="h")
+            hidden.append(h)
+            stats = blocks.tile([P, PIECES * 6], F32, name="stats")
+            for c in range(PIECES):
+                product = psum.tile([P, PIECE], F32, name="product")
+                nc.tensor.matmul(
+                    product[:],
+                    w_sb[:, t * P : (t + 1) * P],
+                    table_sb[:].indirect(
+                        offsets[:, c * PIECE_OFFSET_COLUMNS : (c + 1) * PIECE_OFFSET_COLUMNS]
+                    ),
+                    start=True,
+                    stop=True,
+                )
+                h_piece = h[:, c * PIECE : (c + 1) * PIECE]
+                nc.scalar.activation(h_piece, product[:], ACT.Relu, bias=b_sb[:, t : t + 1])
+                nc.vector.bn_stats(stats[:, c * 6 : (c + 1) * 6], h_piece)
+            nc.vector.bn_aggr(mean_var[:, t, :], stats[:])
+
+        mean = mean_var[:, :, 0]
+        var = mean_var[:, :, 1]
+        inverse_std = held.tile([P, BLOCKS], F32, name="inverse_std")
+        nc.scalar.activation(inverse_std[:], var, ACT.Abs_reciprocal_sqrt, bias=eps[:])
+        slope = held.tile([P, BLOCKS], F32, name="slope")
+        nc.vector.tensor_mul(slope[:], inverse_std[:], gain_sb[:])
+        mean_slope = held.tile([P, BLOCKS], F32, name="mean_slope")
+        nc.vector.tensor_mul(mean_slope[:], mean, slope[:])
+        offset = held.tile([P, BLOCKS], F32, name="offset")
+        nc.vector.tensor_sub(offset[:], shift_sb[:], mean_slope[:])
 
         for t in range(BLOCKS):
-            product = psum.tile([P, N], F32, name="product")
-            nc.tensor.matmul(
-                product[:],
-                w_sb[:, t * P : (t + 1) * P],
-                table_sb[:].indirect(offsets[:]),
-                start=True,
-                stop=True,
+            h = hidden[t]
+            y = blocks.tile([P, N], F32, name="y")
+            nc.vector.tensor_scalar(
+                y[:, :VECTOR_COLUMNS],
+                h[:, :VECTOR_COLUMNS],
+                slope[:, t : t + 1],
+                offset[:, t : t + 1],
+                ALU.mult,
+                ALU.add,
             )
-
-            h = work.tile([P, N], F32, name="h")
-            nc.scalar.activation(h[:], product[:], ACT.Relu, bias=b_sb[:, t : t + 1])
-
-            stats = work.tile([P, 6], F32, name="stats")
-            nc.vector.bn_stats(stats[:], h[:])
-            mean_var = work.tile([P, 2], F32, name="mean_var")
-            nc.vector.bn_aggr(mean_var[:], stats[:])
-            mean = mean_var[:, 0:1]
-            var = mean_var[:, 1:2]
-
-            std = work.tile([P, 1], F32, name="std")
-            nc.scalar.activation(std[:], var, ACT.Sqrt, bias=eps[:])
-            slope = work.tile([P, 1], F32, name="slope")
-            nc.vector.reciprocal(slope[:], std[:])
-            nc.vector.tensor_mul(slope[:], slope[:], gain_sb[:, t : t + 1])
-            drop = work.tile([P, 1], F32, name="drop")
-            nc.vector.scalar_tensor_tensor(
-                drop[:], mean, slope[:], shift_sb[:, t : t + 1], ALU.mult, ALU.subtract
+            nc.scalar.activation(
+                y[:, VECTOR_COLUMNS:],
+                h[:, VECTOR_COLUMNS:],
+                ACT.Identity,
+                bias=offset[:, t : t + 1],
+                scale=slope[:, t : t + 1],
             )
-            y = work.tile([P, N], F32, name="y")
-            nc.vector.tensor_scalar(y[:], h[:], slope[:], drop[:], ALU.mult, ALU.subtract)
             nc.sync.dma_start(out[t * P : (t + 1) * P, :], y[:])

@@ -15,6 +15,7 @@ PIECES = 2
 PIECE = N // PIECES
 PIECE_OFFSET_COLUMNS = PIECE // 16
 BN_EPS = 1e-5
+WARM_UP_MATMULS = 6
 VECTOR_COLUMNS = (2 * N // 3) // 16 * 16
 
 FLOPS = 2 * P * M * N
@@ -26,7 +27,14 @@ def tile_criteomlp_kernel(tc, table, w, b, gain, shift, offs, out):
         tc.tile_pool(name="held", bufs=1) as held,
         tc.tile_pool(name="blocks", bufs=BLOCKS) as blocks,
         tc.psum_pool(name="psum", bufs=BLOCKS * PIECES) as psum,
+        tc.psum_pool(name="unread", bufs=1) as unread,
     ):
+        zeros = held.tile([P, N], BF16, name="zeros")
+        nc.vector.memset(zeros[:], 0.0)
+        zero_product = unread.tile([P, N], F32, name="zero_product")
+        for repeat in range(WARM_UP_MATMULS):
+            nc.tensor.matmul(zero_product[:], zeros[:, :P], zeros[:], start=True, stop=True)
+
         offsets = held.tile([P, N // 16], U16, name="offsets")
         nc.sync.dma_start(offsets[:], offs)
         table_sb = held.tile([P, S], BF16, name="table_sb")

@@ -15,7 +15,6 @@ PIECES = 2
 PIECE = N // PIECES
 PIECE_OFFSET_COLUMNS = PIECE // 16
 BN_EPS = 1e-5
-WARM_UP_MATMULS = 6
 VECTOR_COLUMNS = (2 * N // 3) // 16 * 16
 
 FLOPS = 2 * P * M * N
@@ -27,14 +26,7 @@ def tile_criteomlp_kernel(tc, table, w, b, gain, shift, offs, out):
         tc.tile_pool(name="held", bufs=1) as held,
         tc.tile_pool(name="blocks", bufs=BLOCKS) as blocks,
         tc.psum_pool(name="psum", bufs=BLOCKS * PIECES) as psum,
-        tc.psum_pool(name="unread", bufs=1) as unread,
     ):
-        zeros = held.tile([P, N], BF16, name="zeros")
-        nc.vector.memset(zeros[:], 0.0)
-        zero_product = unread.tile([P, N], F32, name="zero_product")
-        for repeat in range(WARM_UP_MATMULS):
-            nc.tensor.matmul(zero_product[:], zeros[:, :P], zeros[:], start=True, stop=True)
-
         offsets = held.tile([P, N // 16], U16, name="offsets")
         nc.sync.dma_start(offsets[:], offs)
         table_sb = held.tile([P, S], BF16, name="table_sb")
@@ -57,10 +49,9 @@ def tile_criteomlp_kernel(tc, table, w, b, gain, shift, offs, out):
         nc.scalar.activation(first_call[:], eps[:], ACT.Abs_reciprocal_sqrt)
 
         mean_var = held.tile([P, BLOCKS, 2], F32, name="mean_var")
-        hidden = []
+        centred_blocks = []
         for t in range(BLOCKS):
             h = blocks.tile([P, N], F32, name="h")
-            hidden.append(h)
             stats = blocks.tile([P, PIECES * 6], F32, name="stats")
             for c in range(PIECES):
                 product = psum.tile([P, PIECE], F32, name="product")
@@ -77,34 +68,31 @@ def tile_criteomlp_kernel(tc, table, w, b, gain, shift, offs, out):
                 nc.scalar.activation(h_piece, product[:], ACT.Relu, bias=b_sb[:, t : t + 1])
                 nc.vector.bn_stats(stats[:, c * 6 : (c + 1) * 6], h_piece)
             nc.vector.bn_aggr(mean_var[:, t, :], stats[:])
+            centred = blocks.tile([P, N], F32, name="centred")
+            centred_blocks.append(centred)
+            nc.vector.tensor_scalar(
+                centred[:], h[:], mean_var[:, t, 0:1], gain_sb[:, t : t + 1], ALU.subtract, ALU.mult
+            )
 
-        mean = mean_var[:, :, 0]
-        var = mean_var[:, :, 1]
         inverse_std = held.tile([P, BLOCKS], F32, name="inverse_std")
-        nc.scalar.activation(inverse_std[:], var, ACT.Abs_reciprocal_sqrt, bias=eps[:])
-        slope = held.tile([P, BLOCKS], F32, name="slope")
-        nc.vector.tensor_mul(slope[:], inverse_std[:], gain_sb[:])
-        mean_slope = held.tile([P, BLOCKS], F32, name="mean_slope")
-        nc.vector.tensor_mul(mean_slope[:], mean, slope[:])
-        offset = held.tile([P, BLOCKS], F32, name="offset")
-        nc.vector.tensor_sub(offset[:], shift_sb[:], mean_slope[:])
+        nc.scalar.activation(inverse_std[:], mean_var[:, :, 1], ACT.Abs_reciprocal_sqrt, bias=eps[:])
 
         for t in range(BLOCKS):
-            h = hidden[t]
+            centred = centred_blocks[t]
             y = blocks.tile([P, N], F32, name="y")
             nc.vector.tensor_scalar(
                 y[:, :VECTOR_COLUMNS],
-                h[:, :VECTOR_COLUMNS],
-                slope[:, t : t + 1],
-                offset[:, t : t + 1],
+                centred[:, :VECTOR_COLUMNS],
+                inverse_std[:, t : t + 1],
+                shift_sb[:, t : t + 1],
                 ALU.mult,
                 ALU.add,
             )
             nc.scalar.activation(
                 y[:, VECTOR_COLUMNS:],
-                h[:, VECTOR_COLUMNS:],
+                centred[:, VECTOR_COLUMNS:],
                 ACT.Identity,
-                bias=offset[:, t : t + 1],
-                scale=slope[:, t : t + 1],
+                bias=shift_sb[:, t : t + 1],
+                scale=inverse_std[:, t : t + 1],
             )
             nc.sync.dma_start(out[t * P : (t + 1) * P, :], y[:])

@@ -48,8 +48,6 @@ def tile_criteomlp_kernel(tc, table, w, b, gain, shift, offs, out):
         first_call = held.tile([P, 1], F32, name="first_call")
         nc.scalar.activation(first_call[:], eps[:], ACT.Abs_reciprocal_sqrt)
 
-        mean_var = held.tile([P, BLOCKS, 2], F32, name="mean_var")
-        centred_blocks = []
         for t in range(BLOCKS):
             h = blocks.tile([P, N], F32, name="h")
             stats = blocks.tile([P, PIECES * 6], F32, name="stats")
@@ -67,23 +65,21 @@ def tile_criteomlp_kernel(tc, table, w, b, gain, shift, offs, out):
                 h_piece = h[:, c * PIECE : (c + 1) * PIECE]
                 nc.scalar.activation(h_piece, product[:], ACT.Relu, bias=b_sb[:, t : t + 1])
                 nc.vector.bn_stats(stats[:, c * 6 : (c + 1) * 6], h_piece)
-            nc.vector.bn_aggr(mean_var[:, t, :], stats[:])
+            mean_var = blocks.tile([P, 2], F32, name="mean_var")
+            nc.vector.bn_aggr(mean_var[:], stats[:])
+
             centred = blocks.tile([P, N], F32, name="centred")
-            centred_blocks.append(centred)
             nc.vector.tensor_scalar(
-                centred[:], h[:], mean_var[:, t, 0:1], gain_sb[:, t : t + 1], ALU.subtract, ALU.mult
+                centred[:], h[:], mean_var[:, 0:1], gain_sb[:, t : t + 1], ALU.subtract, ALU.mult
             )
+            inverse_std = blocks.tile([P, 1], F32, name="inverse_std")
+            nc.scalar.activation(inverse_std[:], mean_var[:, 1:2], ACT.Abs_reciprocal_sqrt, bias=eps[:])
 
-        inverse_std = held.tile([P, BLOCKS], F32, name="inverse_std")
-        nc.scalar.activation(inverse_std[:], mean_var[:, :, 1], ACT.Abs_reciprocal_sqrt, bias=eps[:])
-
-        for t in range(BLOCKS):
-            centred = centred_blocks[t]
             y = blocks.tile([P, N], F32, name="y")
             nc.vector.tensor_scalar(
                 y[:, :VECTOR_COLUMNS],
                 centred[:, :VECTOR_COLUMNS],
-                inverse_std[:, t : t + 1],
+                inverse_std[:],
                 shift_sb[:, t : t + 1],
                 ALU.mult,
                 ALU.add,
@@ -93,6 +89,6 @@ def tile_criteomlp_kernel(tc, table, w, b, gain, shift, offs, out):
                 centred[:, VECTOR_COLUMNS:],
                 ACT.Identity,
                 bias=shift_sb[:, t : t + 1],
-                scale=inverse_std[:, t : t + 1],
+                scale=inverse_std[:],
             )
             nc.sync.dma_start(out[t * P : (t + 1) * P, :], y[:])

@@ -11,7 +11,7 @@ S = 1024
 M = 256
 N = 512
 BLOCKS = M // P
-PIECES = 2
+PIECES = 4
 PIECE = N // PIECES
 PIECE_OFFSET_COLUMNS = PIECE // 16
 BN_EPS = 1e-5

@@ -14,6 +14,7 @@ BLOCKS = M // P
 PIECES = 4
 PIECE = N // PIECES
 PIECE_OFFSET_COLUMNS = PIECE // 16
+PIECES_IN_A_TURN = 2
 BN_EPS = 1e-5
 VECTOR_COLUMNS = (2 * N // 3) // 16 * 16
 
@@ -48,29 +49,32 @@ def tile_criteomlp_kernel(tc, table, w, b, gain, shift, offs, out):
         first_call = held.tile([P, 1], F32, name="first_call")
         nc.scalar.activation(first_call[:], eps[:], ACT.Abs_reciprocal_sqrt)
 
+        h = [blocks.tile([P, N], F32, name="h") for t in range(BLOCKS)]
+        stats = [blocks.tile([P, PIECES * 6], F32, name="stats") for t in range(BLOCKS)]
+        for turn in range(0, PIECES, PIECES_IN_A_TURN):
+            for t in range(BLOCKS):
+                for c in range(turn, turn + PIECES_IN_A_TURN):
+                    product = psum.tile([P, PIECE], F32, name="product")
+                    nc.tensor.matmul(
+                        product[:],
+                        w_sb[:, t * P : (t + 1) * P],
+                        table_sb[:].indirect(
+                            offsets[:, c * PIECE_OFFSET_COLUMNS : (c + 1) * PIECE_OFFSET_COLUMNS]
+                        ),
+                        start=True,
+                        stop=True,
+                    )
+                    h_piece = h[t][:, c * PIECE : (c + 1) * PIECE]
+                    nc.scalar.activation(h_piece, product[:], ACT.Relu, bias=b_sb[:, t : t + 1])
+                    nc.vector.bn_stats(stats[t][:, c * 6 : (c + 1) * 6], h_piece)
+
         for t in range(BLOCKS):
-            h = blocks.tile([P, N], F32, name="h")
-            stats = blocks.tile([P, PIECES * 6], F32, name="stats")
-            for c in range(PIECES):
-                product = psum.tile([P, PIECE], F32, name="product")
-                nc.tensor.matmul(
-                    product[:],
-                    w_sb[:, t * P : (t + 1) * P],
-                    table_sb[:].indirect(
-                        offsets[:, c * PIECE_OFFSET_COLUMNS : (c + 1) * PIECE_OFFSET_COLUMNS]
-                    ),
-                    start=True,
-                    stop=True,
-                )
-                h_piece = h[:, c * PIECE : (c + 1) * PIECE]
-                nc.scalar.activation(h_piece, product[:], ACT.Relu, bias=b_sb[:, t : t + 1])
-                nc.vector.bn_stats(stats[:, c * 6 : (c + 1) * 6], h_piece)
             mean_var = blocks.tile([P, 2], F32, name="mean_var")
-            nc.vector.bn_aggr(mean_var[:], stats[:])
+            nc.vector.bn_aggr(mean_var[:], stats[t][:])
 
             centred = blocks.tile([P, N], F32, name="centred")
             nc.vector.tensor_scalar(
-                centred[:], h[:], mean_var[:, 0:1], gain_sb[:, t : t + 1], ALU.subtract, ALU.mult
+                centred[:], h[t][:], mean_var[:, 0:1], gain_sb[:, t : t + 1], ALU.subtract, ALU.mult
             )
             inverse_std = blocks.tile([P, 1], F32, name="inverse_std")
             nc.scalar.activation(inverse_std[:], mean_var[:, 1:2], ACT.Abs_reciprocal_sqrt, bias=eps[:])

@@ -38,10 +38,11 @@ def tile_criteomlp_kernel(tc, table, w, b, gain, shift, offs, out):
         b_sb = held.tile([P, BLOCKS], F32, name="b_sb")
         gain_sb = held.tile([P, BLOCKS], F32, name="gain_sb")
         shift_sb = held.tile([P, BLOCKS], F32, name="shift_sb")
-        with nc.allow_non_contiguous_dma(reason="one float32 to a partition, 256 in all"):
-            nc.scalar.dma_start(b_sb[:], b.rearrange("(t p) o -> p (t o)", p=P))
-            nc.scalar.dma_start(gain_sb[:], gain.rearrange("(t p) o -> p (t o)", p=P))
-            nc.scalar.dma_start(shift_sb[:], shift.rearrange("(t p) o -> p (t o)", p=P))
+        nc.scalar.dma_start(b_sb[:], b.rearrange("(p t) o -> p (t o)", t=BLOCKS))
+        nc.scalar.dma_start(gain_sb[:], gain.rearrange("(p t) o -> p (t o)", t=BLOCKS))
+        nc.scalar.dma_start(shift_sb[:], shift.rearrange("(p t) o -> p (t o)", t=BLOCKS))
+        block_weights = w_sb[:].rearrange("k (p t) -> k t p", t=BLOCKS)
+        block_out = out.rearrange("(p t) n -> p t n", t=BLOCKS)
 
         eps = held.tile([P, 1], F32, name="eps")
         nc.vector.memset(eps[:], BN_EPS)
@@ -57,7 +58,7 @@ def tile_criteomlp_kernel(tc, table, w, b, gain, shift, offs, out):
                     product = psum.tile([P, PIECE], F32, name="product")
                     nc.tensor.matmul(
                         product[:],
-                        w_sb[:, t * P : (t + 1) * P],
+                        block_weights[:, t, :],
                         table_sb[:].indirect(
                             offsets[:, c * PIECE_OFFSET_COLUMNS : (c + 1) * PIECE_OFFSET_COLUMNS]
                         ),
@@ -95,4 +96,4 @@ def tile_criteomlp_kernel(tc, table, w, b, gain, shift, offs, out):
                 bias=shift_sb[:, t : t + 1],
                 scale=inverse_std[:],
             )
-            nc.sync.dma_start(out[t * P : (t + 1) * P, :], y[:])
+            nc.sync.dma_start(block_out[:, t, :], y[:])

@@ -39,8 +39,8 @@ def tile_criteomlp_kernel(tc, table, w, b, gain, shift, offs, out):
         gain_sb = held.tile([P, BLOCKS], F32, name="gain_sb")
         shift_sb = held.tile([P, BLOCKS], F32, name="shift_sb")
         nc.scalar.dma_start(b_sb[:], b.rearrange("(p t) o -> p (t o)", t=BLOCKS))
-        nc.scalar.dma_start(gain_sb[:], gain.rearrange("(p t) o -> p (t o)", t=BLOCKS))
-        nc.scalar.dma_start(shift_sb[:], shift.rearrange("(p t) o -> p (t o)", t=BLOCKS))
+        nc.sync.dma_start(gain_sb[:], gain.rearrange("(p t) o -> p (t o)", t=BLOCKS))
+        nc.sync.dma_start(shift_sb[:], shift.rearrange("(p t) o -> p (t o)", t=BLOCKS))
         block_weights = w_sb[:].rearrange("k (p t) -> k t p", t=BLOCKS)
         block_out = out.rearrange("(p t) n -> p t n", t=BLOCKS)
 

import concourse.mybir as mybir

F32 = mybir.dt.float32
BF16 = mybir.dt.bfloat16
U16 = mybir.dt.uint16
ACT = mybir.ActivationFunctionType
ALU = mybir.AluOpType

P = 128
S = 1024
M = 256
N = 512
BLOCKS = M // P
PIECES = 4
PIECE = N // PIECES
PIECE_OFFSET_COLUMNS = PIECE // 16
PIECES_IN_A_TURN = 2
BN_EPS = 1e-5
VECTOR_COLUMNS = (2 * N // 3) // 16 * 16

FLOPS = 2 * P * M * N


def tile_criteomlp_kernel(tc, table, w, b, gain, shift, offs, out):
    nc = tc.nc
    with (
        tc.tile_pool(name="held", bufs=1) as held,
        tc.tile_pool(name="blocks", bufs=BLOCKS) as blocks,
        tc.psum_pool(name="psum", bufs=BLOCKS * PIECES) as psum,
    ):
        offsets = held.tile([P, N // 16], U16, name="offsets")
        nc.sync.dma_start(offsets[:], offs)
        table_sb = held.tile([P, S], BF16, name="table_sb")
        nc.sync.dma_start(table_sb[:], table)
        w_sb = held.tile([P, M], BF16, name="w_sb")
        nc.scalar.dma_start(w_sb[:], w)

        b_sb = held.tile([P, BLOCKS], F32, name="b_sb")
        gain_sb = held.tile([P, BLOCKS], F32, name="gain_sb")
        shift_sb = held.tile([P, BLOCKS], F32, name="shift_sb")
        nc.scalar.dma_start(b_sb[:], b.rearrange("(p t) o -> p (t o)", t=BLOCKS))
        nc.sync.dma_start(gain_sb[:], gain.rearrange("(p t) o -> p (t o)", t=BLOCKS))
        nc.sync.dma_start(shift_sb[:], shift.rearrange("(p t) o -> p (t o)", t=BLOCKS))
        block_weights = w_sb[:].rearrange("k (p t) -> k t p", t=BLOCKS)
        block_out = out.rearrange("(p t) n -> p t n", t=BLOCKS)

        eps = held.tile([P, 1], F32, name="eps")
        nc.vector.memset(eps[:], BN_EPS)

        first_call = held.tile([P, 1], F32, name="first_call")
        nc.scalar.activation(first_call[:], eps[:], ACT.Abs_reciprocal_sqrt)

        h = [blocks.tile([P, N], F32, name="h") for t in range(BLOCKS)]
        stats = [blocks.tile([P, PIECES * 6], F32, name="stats") for t in range(BLOCKS)]
        for turn in range(0, PIECES, PIECES_IN_A_TURN):
            for t in range(BLOCKS):
                for c in range(turn, turn + PIECES_IN_A_TURN):
                    product = psum.tile([P, PIECE], F32, name="product")
                    nc.tensor.matmul(
                        product[:],
                        block_weights[:, t, :],
                        table_sb[:].indirect(
                            offsets[:, c * PIECE_OFFSET_COLUMNS : (c + 1) * PIECE_OFFSET_COLUMNS]
                        ),
                        start=True,
                        stop=True,
                    )
                    h_piece = h[t][:, c * PIECE : (c + 1) * PIECE]
                    nc.scalar.activation(h_piece, product[:], ACT.Relu, bias=b_sb[:, t : t + 1])
                    nc.vector.bn_stats(stats[t][:, c * 6 : (c + 1) * 6], h_piece)

        for t in range(BLOCKS):
            mean_var = blocks.tile([P, 2], F32, name="mean_var")
            nc.vector.bn_aggr(mean_var[:], stats[t][:])

            centred = blocks.tile([P, N], F32, name="centred")
            nc.vector.tensor_scalar(
                centred[:], h[t][:], mean_var[:, 0:1], gain_sb[:, t : t + 1], ALU.subtract, ALU.mult
            )
            inverse_std = blocks.tile([P, 1], F32, name="inverse_std")
            nc.scalar.activation(inverse_std[:], mean_var[:, 1:2], ACT.Abs_reciprocal_sqrt, bias=eps[:])

            y = blocks.tile([P, N], F32, name="y")
            nc.vector.tensor_scalar(
                y[:, :VECTOR_COLUMNS],
                centred[:, :VECTOR_COLUMNS],
                inverse_std[:],
                shift_sb[:, t : t + 1],
                ALU.mult,
                ALU.add,
            )
            nc.scalar.activation(
                y[:, VECTOR_COLUMNS:],
                centred[:, VECTOR_COLUMNS:],
                ACT.Identity,
                bias=shift_sb[:, t : t + 1],
                scale=inverse_std[:],
            )
            nc.sync.dma_start(block_out[:, t, :], y[:])
